import numpy as np
import ml_dtypes


def mxq(x, axis, fmt="e4m3"):
    dtype, down = {"e4m3": (ml_dtypes.float8_e4m3fn, 7), "e5m2": (ml_dtypes.float8_e5m2, 14)}[fmt]
    v = np.moveaxis(np.asarray(x, np.float32).astype(ml_dtypes.bfloat16).astype(np.float64), axis, -1)
    blocks = v.reshape(v.shape[:-1] + (-1, 32))
    amax = np.abs(blocks).max(-1, keepdims=True)
    byte = np.maximum(np.where(amax > 0, np.frexp(amax)[1] - 1 + 127, 0) - down, 1)
    scale = np.exp2(byte - 127.0)
    codes = (blocks / scale).astype(np.float32).astype(dtype).astype(np.float64)
    return np.moveaxis((codes * scale).reshape(v.shape), -1, axis)


WIDE = False


def mx_kscale(k):
    if not WIDE:
        return np.ones(k)
    levels = np.array([10, -10, 5, -5, 0])
    if k % 512:
        return np.exp2(np.random.permutation(np.resize(levels, k // 32))).repeat(32)
    a = np.empty((k // 512, 16))
    for p in range(k // 512):
        a[p, :8] = np.random.permutation(np.resize(levels, 8))
        for g in range(8):
            far = levels[np.abs(levels - a[p, g]) >= 10]
            a[p, g + 8] = far[np.random.randint(len(far))]
    return np.exp2(a.ravel()).repeat(32)


BF16 = ml_dtypes.bfloat16


def bf(x):
    return np.asarray(x, np.float32).astype(BF16)


def f64(x):
    return np.asarray(x).astype(np.float64)


B, S, D, H, HD, P = 4, 2048, 512, 2, 128, 512
N = H * HD
THETA = 500000.0


def rope(t, cos, sin):
    tr = t[..., 0::2]
    ti = t[..., 1::2]
    c = cos[None, :, None, :]
    s = sin[None, :, None, :]
    out = np.stack([tr * c - ti * s, tr * s + ti * c], axis=-1)
    return out.reshape(t.shape)


def draw0():
    s = mx_kscale(D)
    inv = 1.0 / THETA ** (np.arange(0, HD, 2) / HD)
    ang = np.outer(np.arange(S), inv)
    return {"x": bf(np.random.standard_normal((B, S, D)) * s),
            "wq": bf(np.random.standard_normal((N, D)) / np.sqrt(D) / s[None, :]),
            "wk": bf(np.random.standard_normal((N, D)) / np.sqrt(D) / s[None, :]),
            "freqs_cos": bf(np.cos(ang)),
            "freqs_sin": bf(np.sin(ang))}


def core(x, wq, wk, freqs_cos, freqs_sin):
    xm = mxq(f64(x), 2, "e4m3")
    xq = (xm @ mxq(f64(wq), 1, "e4m3").T).reshape(B, S, H, HD)
    xk = (xm @ mxq(f64(wk), 1, "e4m3").T).reshape(B, S, H, HD)
    q = rope(xq, f64(freqs_cos), f64(freqs_sin)).transpose(0, 2, 1, 3)
    k = rope(xk, f64(freqs_cos), f64(freqs_sin)).transpose(0, 2, 1, 3)
    return q, k


def e4m3fn_bytes(y):
    return np.clip(np.asarray(y, np.float64), -448.0, 448.0).astype(np.float32).astype(ml_dtypes.float8_e4m3fn).view(np.uint8)


def e4m3fn_values(b):
    return np.asarray(b, np.uint8).view(ml_dtypes.float8_e4m3fn).astype(np.float64)


def setup_inputs():
    d = draw0()
    x0 = np.asarray(d['x']).astype(np.float64)
    s = (np.max(np.abs(x0), axis=(0, 1), keepdims=True) / 448.0).astype(np.float32)
    out = {}
    for k, v in d.items():
        if k == 'x':
            out['x_bytes'] = e4m3fn_bytes(x0 / s.astype(np.float64))
            out['x_scale'] = s
        else:
            out[k] = v
    return out


def reference(x_bytes, x_scale, wq, wk, freqs_cos, freqs_sin):
    return core(e4m3fn_values(x_bytes) * x_scale.astype(np.float64), wq, wk, freqs_cos, freqs_sin)

@@ -1,0 +1,311 @@
+from contextlib import ExitStack
+
+import concourse.masks as masks
+import concourse.mybir as mybir
+
+F32 = mybir.dt.float32
+BF16 = mybir.dt.bfloat16
+U32 = mybir.dt.uint32
+U8 = mybir.dt.uint8
+FP8 = mybir.dt.float8_e4m3fn
+FP8X4 = mybir.dt.float8_e4m3fn_x4
+ALU = mybir.AluOpType
+COPY = mybir.ActivationFunctionType.Copy
+
+B, S, D = 4, 2048, 512
+P = 128
+JT = S // P
+GT = 4
+NJQ = JT // GT
+FLOPS = 2 * B * S * D * 512
+
+
+def tile_attention_pa_t_kernel(tc, x_bytes, x_scale, wq, wk, freqs_cos, freqs_sin, out_0, out_1):
+    nc = tc.nc
+    outs = (out_0, out_1)
+    groups = [(jq, b) for jq in range(NJQ) for b in range(B)]
+    ng = len(groups)
+
+    with ExitStack() as ctx:
+        const = ctx.enter_context(tc.tile_pool(name="const", bufs=1))
+        bytes_pool = ctx.enter_context(tc.tile_pool(name="bytes", bufs=ng))
+        xb_pool = ctx.enter_context(tc.tile_pool(name="xb", bufs=6))
+        pl_pool = ctx.enter_context(tc.tile_pool(name="pl", bufs=2))
+        xg_pool = ctx.enter_context(tc.tile_pool(name="xg", bufs=2))
+        xq_pool = ctx.enter_context(tc.tile_pool(name="xq", bufs=3))
+        pm_pool = ctx.enter_context(tc.tile_pool(name="pm", bufs=3))
+        p1_pool = ctx.enter_context(tc.tile_pool(name="p1", bufs=3))
+        ost_pool = ctx.enter_context(tc.tile_pool(name="ost", bufs=3))
+        xt_psum = ctx.enter_context(tc.psum_pool(name="xtp", bufs=1))
+        tp_psum = ctx.enter_context(tc.psum_pool(name="tpp", bufs=4))
+        up_psum = ctx.enter_context(tc.psum_pool(name="upp", bufs=2))
+        ctx.enter_context(tc.manual_schedule())
+
+        x_tiles = []
+
+        def load(gi, pieces):
+            jq, b = groups[gi]
+            x8 = bytes_pool.tile([P, GT, D], U8, name="x8", tag="x8")
+            step = GT // pieces
+            for c in range(pieces):
+                nc.sync.dma_start(
+                    out=x8[:, step * c : step * (c + 1), :],
+                    in_=x_bytes[b].rearrange("(p j) k -> p j k", j=JT)[
+                        :, GT * jq + step * c : GT * jq + step * (c + 1), :
+                    ],
+                )
+            x_tiles.append(x8)
+
+        load(0, 2)
+        scl = const.tile([P, 4], F32, name="scl")
+        nc.sync.dma_start(out=scl[:], in_=x_scale.rearrange("a b (p t) -> p (a b t)", t=4))
+        w_ld = const.tile([P, 2, 2, D], BF16, name="w_ld")
+        nc.sync.dma_start(out=w_ld[:, 0], in_=wq.rearrange("(p par) k -> p par k", par=2))
+        nc.sync.dma_start(out=w_ld[:, 1], in_=wk.rearrange("(p par) k -> p par k", par=2))
+        load(1, 1)
+        cosb = const.tile([P, JT, 64], BF16, name="cosb")
+        sinb = const.tile([P, JT, 64], BF16, name="sinb")
+        nc.sync.dma_start(out=cosb[:], in_=freqs_cos.rearrange("(p j) i -> p j i", j=JT))
+        nc.sync.dma_start(out=sinb[:], in_=freqs_sin.rearrange("(p j) i -> p j i", j=JT))
+        for gi in range(2, ng):
+            load(gi, 1)
+
+        ident = const.tile([P, P], F32, name="ident")
+        masks.make_identity(nc, ident[:])
+
+        xb_tiles = {}
+        xt_tiles = {}
+        xg_tiles = {}
+        xq_tiles = {}
+        tp_tiles = {}
+        up_tiles = {}
+        p1_tiles = {}
+        ost_tiles = {}
+        pm_tiles = {}
+
+        def live(gi):
+            return 0 <= gi < ng
+
+        def on_scalar(gi, pr):
+            return pr == 1 and gi >= 2
+
+        def cast(gi, pr):
+            if not live(gi):
+                return
+            xb = xb_pool.tile([P, 2, D], BF16, name="xb", tag="xb")
+            nc.scalar.copy(
+                out=xb[:].rearrange("p j k -> p (j k)"),
+                in_=x_tiles[gi][:, 2 * pr : 2 * pr + 2, :].rearrange("p j k -> p (j k)").bitcast(FP8),
+            )
+            xb_tiles[(gi, pr)] = xb
+
+        def transpose(gi, pr):
+            if not live(gi):
+                return
+            words = xb_tiles[(gi, pr)][:].rearrange("p j k -> p (j k)").bitcast(F32)
+            xt = xt_psum.tile([P, 2, 2, P], F32, name="xt%d" % pr, tag="xt%d" % pr)
+            for jp in range(2):
+                for u in range(2):
+                    nc.tensor.transpose(xt[:, u, jp, :], words[:, 256 * jp + u : 256 * (jp + 1) : 2], ident[:])
+            xt_tiles[(gi, pr)] = xt
+
+        def scale_out(gi, pr):
+            if not live(gi):
+                return
+            if gi not in xg_tiles:
+                xg_new = xg_pool.tile([P, GT, P, 4], BF16, name="xg", tag="xg", align_bytes=64)
+                xg_tiles[gi] = xg_new
+            xg = xg_tiles[gi]
+            xt = xt_tiles[(gi, pr)]
+            src = xt[:].rearrange("p u j r -> p u (j r)").bitcast(BF16).rearrange("p u (c e) -> p u c e", e=2)
+            dst = xg[:, 2 * pr : 2 * pr + 2, :, :].rearrange("p j r t -> p (j r) t")
+            if on_scalar(gi, pr):
+                pl = pl_pool.tile([P, 4, 2 * P], BF16, name="pl", tag="pl")
+                for t in range(4):
+                    nc.scalar.activation(
+                        out=pl[:, t, :], in_=src[:, t // 2, :, t % 2], func=COPY, scale=scl[:, t : t + 1]
+                    )
+                nc.scalar.copy(out=dst, in_=pl[:].rearrange("p t c -> p c t"))
+            else:
+                nc.vector.tensor_tensor(
+                    out=dst.rearrange("p c (u e) -> p c u e", e=2),
+                    in0=src.rearrange("p u c e -> p c u e"),
+                    in1=scl[:].rearrange("p (u e) -> p u e", e=2).unsqueeze(1).to_broadcast([P, 2 * P, 2, 2]),
+                    op=ALU.mult,
+                )
+
+        def quantize(gi):
+            if not live(gi):
+                return
+            xc = xq_pool.tile([P, GT * P], U32, name="xc", tag="xc", align_bytes=64)
+            xs = xq_pool.tile([P, GT * P], U8, name="xs", tag="xs", align_bytes=64)
+            nc.vector.quantize_mx(
+                out=xc[:].bitcast(FP8X4),
+                scales=xs[:],
+                in_=xg_tiles[gi][:].rearrange("p j r t -> p (j r t)"),
+            )
+            xq_tiles[gi] = (xc, xs)
+
+        def multiply_sum(gi, pr):
+            if not live(gi):
+                return
+            xc, xs = xq_tiles[gi]
+            up = up_psum.tile([P, 2, 256], F32, name="up", tag="up")
+            up_tiles[(gi, pr)] = up
+            for jp in range(2):
+                cols = slice(P * (2 * pr + jp), P * (2 * pr + jp + 1))
+                for half in range(2):
+                    nc.tensor.matmul_mx(
+                        out=up[:, jp, :],
+                        lhsT=xc[:, cols].bitcast(FP8X4),
+                        lhsT_scale=xs[:, cols],
+                        rhs=wc[:, 256 * half : 256 * (half + 1)].bitcast(FP8X4),
+                        rhs_scale=ws[:, 256 * half : 256 * (half + 1)],
+                        start=(half == 0),
+                        stop=(half == 1),
+                    )
+
+        def multiply(gi, jj):
+            if not live(gi):
+                return
+            xc, xs = xq_tiles[gi]
+            cols = slice(P * jj, P * (jj + 1))
+            tp = tp_psum.tile([P, 512], F32, name="tp", tag="tp")
+            tp_tiles[(gi, jj)] = tp
+            nc.tensor.matmul_mx(
+                out=tp[:],
+                lhsT=xc[:, cols].bitcast(FP8X4),
+                lhsT_scale=xs[:, cols],
+                rhs=wc[:].bitcast(FP8X4),
+                rhs_scale=ws[:],
+                start=True,
+                stop=True,
+            )
+
+        def shared_product(gi, pr):
+            if not live(gi):
+                return
+            jq, b = groups[gi]
+            j0 = GT * jq + 2 * pr
+            p1 = p1_pool.tile([P, 4, 2, 64], F32, name="p1", tag="p1")
+            nc.vector.tensor_tensor(
+                out=p1[:].rearrange("p g j i -> p j g i"),
+                in0=up_tiles[(gi, pr)][:].rearrange("p j (g i) -> p j g i", g=4),
+                in1=cosb[:, j0 : j0 + 2, :].unsqueeze(2).to_broadcast([P, 2, 4, 64]),
+                op=ALU.mult,
+            )
+            p1_tiles[(gi, pr)] = p1
+
+        def rotate(gi, jj):
+            if not live(gi):
+                return
+            jq, b = groups[gi]
+            width = 2 if gi == ng - 1 else GT
+            if jj % width == 0:
+                ost_new = ost_pool.tile([P, 4, width, P], F32, name="ost", tag="ost")
+                ost_tiles[(gi, jj // width)] = ost_new
+            ost = ost_tiles[(gi, jj // width)]
+            if jj % 2 == 0:
+                pm_new = pm_pool.tile([P, 4, 2, 64, 2], F32, name="pm", tag="pm")
+                pm_tiles[(gi, jj // 2)] = pm_new
+            pm = pm_tiles[(gi, jj // 2)]
+            p1 = p1_tiles[(gi, jj // 2)]
+            nc.vector.tensor_tensor(
+                out=pm[:, :, jj % 2, :, :],
+                in0=tp_tiles[(gi, jj)][:].rearrange("p (q g i) -> p g i q", q=2, g=4),
+                in1=t2[:, :, GT * jq + jj, :].rearrange("p q i -> p i q").unsqueeze(1).to_broadcast([P, 4, 64, 2]),
+                op=ALU.mult,
+            )
+            if gi == ng - 1 and jj >= 2:
+                nc.vector.tensor_tensor(
+                    out=ost[:, :, jj % width, :].rearrange("p g (i q) -> p g i q", q=2),
+                    in0=pm[:, :, jj % 2, :, :],
+                    in1=p1[:, :, jj % 2, :].unsqueeze(3).to_broadcast([P, 4, 64, 2]),
+                    op=ALU.add,
+                )
+            elif jj % 2 == 1:
+                nc.gpsimd.tensor_tensor(
+                    out=ost[:, :, jj % width - 1 : jj % width + 1, :].rearrange("p g j (i q) -> p g (j i) q", q=2),
+                    in0=pm[:].rearrange("p g j i q -> p g (j i) q"),
+                    in1=p1[:].rearrange("p g j i -> p g (j i)").unsqueeze(3).to_broadcast([P, 4, 2 * 64, 2]),
+                    op=ALU.add,
+                )
+
+        def store(gi, j_lo, j_hi):
+            jq, b = groups[gi]
+            ost = ost_tiles[(gi, j_lo // (j_hi - j_lo))]
+            for tn in range(2):
+                nc.sync.dma_start(
+                    out=outs[tn][b].rearrange("h (p j) d -> p h j d", j=JT)[:, :, GT * jq + j_lo : GT * jq + j_hi, :],
+                    in_=ost[:, 2 * tn : 2 * tn + 2, :, :],
+                )
+
+        negc = const.tile([P, JT, 64], F32, name="negc")
+        t2 = const.tile([P, 2, JT, 64], F32, name="t2")
+
+        def tables(jq, eng):
+            js = slice(GT * jq, GT * (jq + 1))
+            eng.tensor_scalar(
+                out=negc[:, js, :], in0=cosb[:, js, :], scalar1=-1.0, scalar2=0.0, op0=ALU.mult, op1=ALU.add
+            )
+            eng.tensor_tensor(out=t2[:, 0, js, :], in0=negc[:, js, :], in1=sinb[:, js, :], op=ALU.subtract)
+            eng.tensor_tensor(out=t2[:, 1, js, :], in0=negc[:, js, :], in1=sinb[:, js, :], op=ALU.add)
+
+        wg = const.tile([P, 512, 4], BF16, name="wg", align_bytes=64)
+        wc = const.tile([P, 512], U32, name="wc", align_bytes=64)
+        ws = const.tile([P, 512], U8, name="ws", align_bytes=64)
+
+        def weights():
+            for q in range(2):
+                wt = tp_psum.tile([P, 2, 256], F32, name="wt", tag="tp")
+                for tn in range(2):
+                    w_words = w_ld[:, tn, 1 - q, :].bitcast(F32)
+                    for u in range(2):
+                        nc.tensor.transpose(wt[:, u, P * tn : P * (tn + 1)], w_words[:, u:256:2], ident[:])
+                nc.scalar.copy(
+                    out=wg[:, 256 * q : 256 * (q + 1), :]
+                    .rearrange("p c t -> p (c t)")
+                    .bitcast(F32)
+                    .rearrange("p (c u) -> p c u", u=2),
+                    in_=wt[:].rearrange("p u c -> p c u"),
+                )
+
+        for jq in range(NJQ):
+            tables(jq, nc.gpsimd)
+
+        for gi in range(-4, ng):
+            if on_scalar(gi + 2, 1):
+                scale_out(gi + 2, 1)
+            cast(gi + 4, 0)
+            cast(gi + 4, 1)
+            if gi == -4:
+                transpose(0, 0)
+                weights()
+                transpose(0, 1)
+            shared_product(gi, 0)
+            multiply_sum(gi + 1, 0)
+            rotate(gi, 0)
+            multiply(gi + 1, 0)
+            rotate(gi, 1)
+            multiply(gi + 1, 1)
+            if gi == ng - 1:
+                store(gi, 0, 2)
+            scale_out(gi + 2, 0)
+            if not on_scalar(gi + 2, 1):
+                scale_out(gi + 2, 1)
+            if gi > -3:
+                transpose(gi + 3, 0)
+                transpose(gi + 3, 1)
+            shared_product(gi, 1)
+            multiply_sum(gi + 1, 1)
+            rotate(gi, 2)
+            multiply(gi + 1, 2)
+            rotate(gi, 3)
+            multiply(gi + 1, 3)
+            if gi == -2:
+                nc.vector.quantize_mx(out=wc[:].bitcast(FP8X4), scales=ws[:], in_=wg[:].rearrange("p c t -> p (c t)"))
+            quantize(gi + 2)
+            if gi == ng - 1:
+                store(gi, 2, 4)
+            elif live(gi):
+                store(gi, 0, GT)

@@ -86,6 +86,9 @@ def tile_attention_pa_t_kernel(tc, x_bytes, x_scale, wq, wk, freqs_cos, freqs_si
         def live(gi):
             return 0 <= gi < ng
 
+        def width(gi):
+            return GT if 0 < gi < ng - 1 else 2
+
         def on_scalar(gi, pr):
             return pr == 1 and gi >= 2
 
@@ -187,47 +190,50 @@ def tile_attention_pa_t_kernel(tc, x_bytes, x_scale, wq, wk, freqs_cos, freqs_si
                 return
             jq, b = groups[gi]
             j0 = GT * jq + 2 * pr
-            p1 = p1_pool.tile([P, 4, 2, 64], F32, name="p1", tag="p1")
+            w = width(gi)
+            if (2 * pr) % w == 0:
+                p1_new = p1_pool.tile([P, 4, w, 64], F32, name="p1", tag="p1")
+                p1_tiles[(gi, 2 * pr // w)] = p1_new
+            p1 = p1_tiles[(gi, 2 * pr // w)]
+            jl = (2 * pr) % w
             nc.vector.tensor_tensor(
-                out=p1[:].rearrange("p g j i -> p j g i"),
+                out=p1[:, :, jl : jl + 2, :].rearrange("p g j i -> p j g i"),
                 in0=up_tiles[(gi, pr)][:].rearrange("p j (g i) -> p j g i", g=4),
                 in1=cosb[:, j0 : j0 + 2, :].unsqueeze(2).to_broadcast([P, 2, 4, 64]),
                 op=ALU.mult,
             )
-            p1_tiles[(gi, pr)] = p1
 
         def rotate(gi, jj):
             if not live(gi):
                 return
             jq, b = groups[gi]
-            width = 2 if gi == ng - 1 else GT
-            if jj % width == 0:
-                ost_new = ost_pool.tile([P, 4, width, P], F32, name="ost", tag="ost")
-                ost_tiles[(gi, jj // width)] = ost_new
-            ost = ost_tiles[(gi, jj // width)]
-            if jj % 2 == 0:
-                pm_new = pm_pool.tile([P, 4, 2, 64, 2], F32, name="pm", tag="pm")
-                pm_tiles[(gi, jj // 2)] = pm_new
-            pm = pm_tiles[(gi, jj // 2)]
-            p1 = p1_tiles[(gi, jj // 2)]
+            w = width(gi)
+            if jj % w == 0:
+                ost_new = ost_pool.tile([P, 4, w, P], F32, name="ost", tag="ost")
+                ost_tiles[(gi, jj // w)] = ost_new
+                pm_new = pm_pool.tile([P, 4, w, 64, 2], F32, name="pm", tag="pm")
+                pm_tiles[(gi, jj // w)] = pm_new
+            ost = ost_tiles[(gi, jj // w)]
+            pm = pm_tiles[(gi, jj // w)]
+            p1 = p1_tiles[(gi, jj // w)]
             nc.vector.tensor_tensor(
-                out=pm[:, :, jj % 2, :, :],
+                out=pm[:, :, jj % w, :, :],
                 in0=tp_tiles[(gi, jj)][:].rearrange("p (q g i) -> p g i q", q=2, g=4),
                 in1=t2[:, :, GT * jq + jj, :].rearrange("p q i -> p i q").unsqueeze(1).to_broadcast([P, 4, 64, 2]),
                 op=ALU.mult,
             )
             if gi == ng - 1 and jj >= 2:
                 nc.vector.tensor_tensor(
-                    out=ost[:, :, jj % width, :].rearrange("p g (i q) -> p g i q", q=2),
-                    in0=pm[:, :, jj % 2, :, :],
-                    in1=p1[:, :, jj % 2, :].unsqueeze(3).to_broadcast([P, 4, 64, 2]),
+                    out=ost[:, :, jj % w, :].rearrange("p g (i q) -> p g i q", q=2),
+                    in0=pm[:, :, jj % w, :, :],
+                    in1=p1[:, :, jj % w, :].unsqueeze(3).to_broadcast([P, 4, 64, 2]),
                     op=ALU.add,
                 )
-            elif jj % 2 == 1:
+            elif jj % w == w - 1:
                 nc.gpsimd.tensor_tensor(
-                    out=ost[:, :, jj % width - 1 : jj % width + 1, :].rearrange("p g j (i q) -> p g (j i) q", q=2),
+                    out=ost[:].rearrange("p g j (i q) -> p g (j i) q", q=2),
                     in0=pm[:].rearrange("p g j i q -> p g (j i) q"),
-                    in1=p1[:].rearrange("p g j i -> p g (j i)").unsqueeze(3).to_broadcast([P, 4, 2 * 64, 2]),
+                    in1=p1[:].rearrange("p g j i -> p g (j i)").unsqueeze(3).to_broadcast([P, 4, w * 64, 2]),
                     op=ALU.add,
                 )
 
@@ -288,7 +294,7 @@ def tile_attention_pa_t_kernel(tc, x_bytes, x_scale, wq, wk, freqs_cos, freqs_si
             multiply(gi + 1, 0)
             rotate(gi, 1)
             multiply(gi + 1, 1)
-            if gi == ng - 1:
+            if live(gi) and width(gi) == 2:
                 store(gi, 0, 2)
             scale_out(gi + 2, 0)
             if not on_scalar(gi + 2, 1):
@@ -305,7 +311,7 @@ def tile_attention_pa_t_kernel(tc, x_bytes, x_scale, wq, wk, freqs_cos, freqs_si
             if gi == -2:
                 nc.vector.quantize_mx(out=wc[:].bitcast(FP8X4), scales=ws[:], in_=wg[:].rearrange("p c t -> p (c t)"))
             quantize(gi + 2)
-            if gi == ng - 1:
+            if live(gi) and width(gi) == 2:
                 store(gi, 2, 4)
             elif live(gi):
                 store(gi, 0, GT)

@@ -33,8 +33,8 @@ def tile_attention_pa_t_kernel(tc, x_bytes, x_scale, wq, wk, freqs_cos, freqs_si
         pl_pool = ctx.enter_context(tc.tile_pool(name="pl", bufs=2))
         xg_pool = ctx.enter_context(tc.tile_pool(name="xg", bufs=2))
         xq_pool = ctx.enter_context(tc.tile_pool(name="xq", bufs=3))
-        pm_pool = ctx.enter_context(tc.tile_pool(name="pm", bufs=3))
-        p1_pool = ctx.enter_context(tc.tile_pool(name="p1", bufs=3))
+        pm_pool = ctx.enter_context(tc.tile_pool(name="pm", bufs=5))
+        p1_pool = ctx.enter_context(tc.tile_pool(name="p1", bufs=5))
         ost_pool = ctx.enter_context(tc.tile_pool(name="ost", bufs=3))
         xt_psum = ctx.enter_context(tc.psum_pool(name="xtp", bufs=1))
         tp_psum = ctx.enter_context(tc.psum_pool(name="tpp", bufs=4))
@@ -80,14 +80,16 @@ def tile_attention_pa_t_kernel(tc, x_bytes, x_scale, wq, wk, freqs_cos, freqs_si
         tp_tiles = {}
         up_tiles = {}
         p1_tiles = {}
-        ost_tiles = {}
         pm_tiles = {}
 
         def live(gi):
             return 0 <= gi < ng
 
         def width(gi):
-            return GT if 0 < gi < ng - 1 else 2
+            return GT if 0 < gi < ng - 2 else 2
+
+        def vector_adds(gi, half):
+            return (gi, half) >= (ng - 2, 1)
 
         def on_scalar(gi, pr):
             return pr == 1 and gi >= 2
@@ -209,37 +211,29 @@ def tile_attention_pa_t_kernel(tc, x_bytes, x_scale, wq, wk, freqs_cos, freqs_si
             jq, b = groups[gi]
             w = width(gi)
             if jj % w == 0:
-                ost_new = ost_pool.tile([P, 4, w, P], F32, name="ost", tag="ost")
-                ost_tiles[(gi, jj // w)] = ost_new
                 pm_new = pm_pool.tile([P, 4, w, 64, 2], F32, name="pm", tag="pm")
                 pm_tiles[(gi, jj // w)] = pm_new
-            ost = ost_tiles[(gi, jj // w)]
             pm = pm_tiles[(gi, jj // w)]
-            p1 = p1_tiles[(gi, jj // w)]
             nc.vector.tensor_tensor(
                 out=pm[:, :, jj % w, :, :],
                 in0=tp_tiles[(gi, jj)][:].rearrange("p (q g i) -> p g i q", q=2, g=4),
                 in1=t2[:, :, GT * jq + jj, :].rearrange("p q i -> p i q").unsqueeze(1).to_broadcast([P, 4, 64, 2]),
                 op=ALU.mult,
             )
-            if gi == ng - 1 and jj >= 2:
-                nc.vector.tensor_tensor(
-                    out=ost[:, :, jj % w, :].rearrange("p g (i q) -> p g i q", q=2),
-                    in0=pm[:, :, jj % w, :, :],
-                    in1=p1[:, :, jj % w, :].unsqueeze(3).to_broadcast([P, 4, 64, 2]),
-                    op=ALU.add,
-                )
-            elif jj % w == w - 1:
-                nc.gpsimd.tensor_tensor(
-                    out=ost[:].rearrange("p g j (i q) -> p g (j i) q", q=2),
-                    in0=pm[:].rearrange("p g j i q -> p g (j i) q"),
-                    in1=p1[:].rearrange("p g j i -> p g (j i)").unsqueeze(3).to_broadcast([P, 4, w * 64, 2]),
-                    op=ALU.add,
-                )
 
-        def store(gi, j_lo, j_hi):
+        def add_and_store(gi, half):
             jq, b = groups[gi]
-            ost = ost_tiles[(gi, j_lo // (j_hi - j_lo))]
+            w = width(gi)
+            ost = ost_pool.tile([P, 4, w, P], F32, name="ost", tag="ost")
+            eng = nc.vector if vector_adds(gi, half) else nc.gpsimd
+            eng.tensor_tensor(
+                out=ost[:].rearrange("p g j (i q) -> p g (j i) q", q=2),
+                in0=pm_tiles[(gi, half)][:].rearrange("p g j i q -> p g (j i) q"),
+                in1=p1_tiles[(gi, half)][:].rearrange("p g j i -> p g (j i)").unsqueeze(3).to_broadcast([P, 4, w * 64, 2]),
+                op=ALU.add,
+            )
+            j_lo = w * half
+            j_hi = w * (half + 1)
             for tn in range(2):
                 nc.sync.dma_start(
                     out=outs[tn][b].rearrange("h (p j) d -> p h j d", j=JT)[:, :, GT * jq + j_lo : GT * jq + j_hi, :],
@@ -294,8 +288,8 @@ def tile_attention_pa_t_kernel(tc, x_bytes, x_scale, wq, wk, freqs_cos, freqs_si
             multiply(gi + 1, 0)
             rotate(gi, 1)
             multiply(gi + 1, 1)
-            if live(gi) and width(gi) == 2:
-                store(gi, 0, 2)
+            if live(gi) and width(gi) == 2 and not vector_adds(gi, 0):
+                add_and_store(gi, 0)
             scale_out(gi + 2, 0)
             if not on_scalar(gi + 2, 1):
                 scale_out(gi + 2, 1)
@@ -311,7 +305,7 @@ def tile_attention_pa_t_kernel(tc, x_bytes, x_scale, wq, wk, freqs_cos, freqs_si
             if gi == -2:
                 nc.vector.quantize_mx(out=wc[:].bitcast(FP8X4), scales=ws[:], in_=wg[:].rearrange("p c t -> p (c t)"))
             quantize(gi + 2)
-            if live(gi) and width(gi) == 2:
-                store(gi, 2, 4)
-            elif live(gi):
-                store(gi, 0, GT)
+            if live(gi) and not vector_adds(gi, GT // width(gi) - 1):
+                add_and_store(gi, GT // width(gi) - 1)
+        for gi, half in ((ng - 2, 1), (ng - 1, 0), (ng - 1, 1)):
+            add_and_store(gi, half)

@@ -98,7 +98,8 @@ def tile_attention_pa_t_kernel(tc, x_bytes, x_scale, wq, wk, freqs_cos, freqs_si
             if not live(gi):
                 return
             xb = xb_pool.tile([P, 2, D], BF16, name="xb", tag="xb")
-            nc.scalar.copy(
+            widen = nc.vector.tensor_copy if gi == 0 else nc.scalar.copy
+            widen(
                 out=xb[:].rearrange("p j k -> p (j k)"),
                 in_=x_tiles[gi][:, 2 * pr : 2 * pr + 2, :].rearrange("p j k -> p (j k)").bitcast(FP8),
             )
@@ -280,8 +281,8 @@ def tile_attention_pa_t_kernel(tc, x_bytes, x_scale, wq, wk, freqs_cos, freqs_si
             cast(gi + 4, 1)
             if gi == -4:
                 transpose(0, 0)
-                weights()
                 transpose(0, 1)
+                weights()
             shared_product(gi, 0)
             multiply_sum(gi + 1, 0)
             rotate(gi, 0)

@@ -35,7 +35,7 @@ def tile_attention_pa_t_kernel(tc, x_bytes, x_scale, wq, wk, freqs_cos, freqs_si
         xq_pool = ctx.enter_context(tc.tile_pool(name="xq", bufs=3))
         pm_pool = ctx.enter_context(tc.tile_pool(name="pm", bufs=5))
         p1_pool = ctx.enter_context(tc.tile_pool(name="p1", bufs=5))
-        ost_pool = ctx.enter_context(tc.tile_pool(name="ost", bufs=3))
+        ost_pool = ctx.enter_context(tc.tile_pool(name="ost", bufs=5))
         xt_psum = ctx.enter_context(tc.psum_pool(name="xtp", bufs=1))
         tp_psum = ctx.enter_context(tc.psum_pool(name="tpp", bufs=4))
         up_psum = ctx.enter_context(tc.psum_pool(name="upp", bufs=2))
@@ -72,6 +72,16 @@ def tile_attention_pa_t_kernel(tc, x_bytes, x_scale, wq, wk, freqs_cos, freqs_si
 
         ident = const.tile([P, P], F32, name="ident")
         masks.make_identity(nc, ident[:])
+
+        dz = const.tile([P, 512], BF16, name="dz")
+        nc.vector.memset(dz[:], 0.0)
+        wp = up_psum.tile([P, 2, 256], F32, name="wp", tag="up")
+
+        def warm(n):
+            for i in range(n):
+                nc.tensor.matmul(
+                    out=wp[:].rearrange("p a b -> p (a b)"), lhsT=dz[:, 0:P], rhs=dz[:], start=True, stop=True
+                )
 
         xb_tiles = {}
         xt_tiles = {}
@@ -280,9 +290,12 @@ def tile_attention_pa_t_kernel(tc, x_bytes, x_scale, wq, wk, freqs_cos, freqs_si
             cast(gi + 4, 0)
             cast(gi + 4, 1)
             if gi == -4:
+                warm(3)
                 transpose(0, 0)
                 transpose(0, 1)
+                warm(2)
                 weights()
+                warm(2)
             shared_product(gi, 0)
             multiply_sum(gi + 1, 0)
             rotate(gi, 0)
@@ -297,6 +310,8 @@ def tile_attention_pa_t_kernel(tc, x_bytes, x_scale, wq, wk, freqs_cos, freqs_si
             if gi > -3:
                 transpose(gi + 3, 0)
                 transpose(gi + 3, 1)
+            if gi == -2:
+                warm(2)
             shared_product(gi, 1)
             multiply_sum(gi + 1, 1)
             rotate(gi, 2)

@@ -239,9 +239,9 @@ def tile_attention_pa_t_kernel(tc, x_bytes, x_scale, wq, wk, freqs_cos, freqs_si
             eng = nc.vector if vector_adds(gi, half) else nc.gpsimd
             eng.tensor_tensor(
                 out=ost[:].rearrange("p g j (i q) -> p g (j i) q", q=2),
-                in0=pm_tiles[(gi, half)][:].rearrange("p g j i q -> p g (j i) q"),
-                in1=p1_tiles[(gi, half)][:].rearrange("p g j i -> p g (j i)").unsqueeze(3).to_broadcast([P, 4, w * 64, 2]),
-                op=ALU.add,
+                in0=p1_tiles[(gi, half)][:].rearrange("p g j i -> p g (j i)").unsqueeze(3).to_broadcast([P, 4, w * 64, 2]),
+                in1=pm_tiles[(gi, half)][:].rearrange("p g j i q -> p g (j i) q"),
+                op=ALU.subtract,
             )
             j_lo = w * half
             j_hi = w * (half + 1)
@@ -251,16 +251,12 @@ def tile_attention_pa_t_kernel(tc, x_bytes, x_scale, wq, wk, freqs_cos, freqs_si
                     in_=ost[:, 2 * tn : 2 * tn + 2, :, :],
                 )
 
-        negc = const.tile([P, JT, 64], F32, name="negc")
         t2 = const.tile([P, 2, JT, 64], F32, name="t2")
 
         def tables(jq, eng):
             js = slice(GT * jq, GT * (jq + 1))
-            eng.tensor_scalar(
-                out=negc[:, js, :], in0=cosb[:, js, :], scalar1=-1.0, scalar2=0.0, op0=ALU.mult, op1=ALU.add
-            )
-            eng.tensor_tensor(out=t2[:, 0, js, :], in0=negc[:, js, :], in1=sinb[:, js, :], op=ALU.subtract)
-            eng.tensor_tensor(out=t2[:, 1, js, :], in0=negc[:, js, :], in1=sinb[:, js, :], op=ALU.add)
+            eng.tensor_tensor(out=t2[:, 0, js, :], in0=cosb[:, js, :], in1=sinb[:, js, :], op=ALU.add)
+            eng.tensor_tensor(out=t2[:, 1, js, :], in0=cosb[:, js, :], in1=sinb[:, js, :], op=ALU.subtract)
 
         wg = const.tile([P, 512, 4], BF16, name="wg", align_bytes=64)
         wc = const.tile([P, 512], U32, name="wc", align_bytes=64)
@@ -287,9 +283,12 @@ def tile_attention_pa_t_kernel(tc, x_bytes, x_scale, wq, wk, freqs_cos, freqs_si
         for gi in range(-4, ng):
             if on_scalar(gi + 2, 1):
                 scale_out(gi + 2, 1)
-            cast(gi + 4, 0)
-            cast(gi + 4, 1)
+            if gi != -3:
+                cast(gi + 4, 0)
+                cast(gi + 4, 1)
             if gi == -4:
+                cast(1, 0)
+                cast(1, 1)
                 warm(3)
                 transpose(0, 0)
                 transpose(0, 1)

@@ -141,7 +141,9 @@ def tile_attention_pa_t_kernel(tc, x_bytes, x_scale, wq, wk, freqs_cos, freqs_si
                     nc.scalar.activation(
                         out=pl[:, t, :], in_=src[:, t // 2, :, t % 2], func=COPY, scale=scl[:, t : t + 1]
                     )
-                nc.scalar.copy(out=dst, in_=pl[:].rearrange("p t c -> p c t"))
+                nc.scalar.copy(
+                    out=dst.rearrange("p (c i) t -> p c t i", i=4), in_=pl[:].rearrange("p t (c i) -> p c t i", i=4)
+                )
             else:
                 nc.vector.tensor_tensor(
                     out=dst.rearrange("p c (u e) -> p c u e", e=2),

@@ -73,16 +73,6 @@ def tile_attention_pa_t_kernel(tc, x_bytes, x_scale, wq, wk, freqs_cos, freqs_si
         ident = const.tile([P, P], F32, name="ident")
         masks.make_identity(nc, ident[:])
 
-        dz = const.tile([P, 512], BF16, name="dz")
-        nc.vector.memset(dz[:], 0.0)
-        wp = up_psum.tile([P, 2, 256], F32, name="wp", tag="up")
-
-        def warm(n):
-            for i in range(n):
-                nc.tensor.matmul(
-                    out=wp[:].rearrange("p a b -> p (a b)"), lhsT=dz[:, 0:P], rhs=dz[:], start=True, stop=True
-                )
-
         xb_tiles = {}
         xt_tiles = {}
         xg_tiles = {}
@@ -291,12 +281,9 @@ def tile_attention_pa_t_kernel(tc, x_bytes, x_scale, wq, wk, freqs_cos, freqs_si
             if gi == -4:
                 cast(1, 0)
                 cast(1, 1)
-                warm(3)
                 transpose(0, 0)
                 transpose(0, 1)
-                warm(2)
                 weights()
-                warm(2)
             shared_product(gi, 0)
             multiply_sum(gi + 1, 0)
             rotate(gi, 0)
@@ -311,8 +298,6 @@ def tile_attention_pa_t_kernel(tc, x_bytes, x_scale, wq, wk, freqs_cos, freqs_si
             if gi > -3:
                 transpose(gi + 3, 0)
                 transpose(gi + 3, 1)
-            if gi == -2:
-                warm(2)
             shared_product(gi, 1)
             multiply_sum(gi + 1, 1)
             rotate(gi, 2)

@@ -98,7 +98,7 @@ def tile_attention_pa_t_kernel(tc, x_bytes, x_scale, wq, wk, freqs_cos, freqs_si
             if not live(gi):
                 return
             xb = xb_pool.tile([P, 2, D], BF16, name="xb", tag="xb")
-            widen = nc.vector.tensor_copy if gi == 0 else nc.scalar.copy
+            widen = nc.vector.tensor_copy if (gi, pr) == (0, 0) else nc.scalar.copy
             widen(
                 out=xb[:].rearrange("p j k -> p (j k)"),
                 in_=x_tiles[gi][:, 2 * pr : 2 * pr + 2, :].rearrange("p j k -> p (j k)").bitcast(FP8),
@@ -238,7 +238,8 @@ def tile_attention_pa_t_kernel(tc, x_bytes, x_scale, wq, wk, freqs_cos, freqs_si
             j_lo = w * half
             j_hi = w * (half + 1)
             for tn in range(2):
-                nc.sync.dma_start(
+                queue = nc.scalar if tn == 1 and vector_adds(gi, half) else nc.sync
+                queue.dma_start(
                     out=outs[tn][b].rearrange("h (p j) d -> p h j d", j=JT)[:, :, GT * jq + j_lo : GT * jq + j_hi, :],
                     in_=ost[:, 2 * tn : 2 * tn + 2, :, :],
                 )

@@ -59,15 +59,22 @@ def tile_attention_pa_t_kernel(tc, x_bytes, x_scale, wq, wk, freqs_cos, freqs_si
         load(0, 2)
         scl = const.tile([P, 4], F32, name="scl")
         nc.sync.dma_start(out=scl[:], in_=x_scale.rearrange("a b (p t) -> p (a b t)", t=4))
+        cosb = const.tile([P, JT, 64], BF16, name="cosb")
+        sinb = const.tile([P, JT, 64], BF16, name="sinb")
+
+        def load_tables(lo, hi):
+            nc.sync.dma_start(out=cosb[:, lo:hi, :], in_=freqs_cos.rearrange("(p j) i -> p j i", j=JT)[:, lo:hi, :])
+            nc.sync.dma_start(out=sinb[:, lo:hi, :], in_=freqs_sin.rearrange("(p j) i -> p j i", j=JT)[:, lo:hi, :])
+
+        load_tables(0, GT)
         w_ld = const.tile([P, 2, 2, D], BF16, name="w_ld")
         nc.sync.dma_start(out=w_ld[:, 0], in_=wq.rearrange("(p par) k -> p par k", par=2))
         nc.sync.dma_start(out=w_ld[:, 1], in_=wk.rearrange("(p par) k -> p par k", par=2))
         load(1, 1)
-        cosb = const.tile([P, JT, 64], BF16, name="cosb")
-        sinb = const.tile([P, JT, 64], BF16, name="sinb")
-        nc.sync.dma_start(out=cosb[:], in_=freqs_cos.rearrange("(p j) i -> p j i", j=JT))
-        nc.sync.dma_start(out=sinb[:], in_=freqs_sin.rearrange("(p j) i -> p j i", j=JT))
-        for gi in range(2, ng):
+        for gi in range(2, 6):
+            load(gi, 1)
+        load_tables(GT, JT)
+        for gi in range(6, ng):
             load(gi, 1)
 
         ident = const.tile([P, P], F32, name="ident")
@@ -246,45 +253,50 @@ def tile_attention_pa_t_kernel(tc, x_bytes, x_scale, wq, wk, freqs_cos, freqs_si
 
         t2 = const.tile([P, 2, JT, 64], F32, name="t2")
 
-        def tables(jq, eng):
-            js = slice(GT * jq, GT * (jq + 1))
-            eng.tensor_tensor(out=t2[:, 0, js, :], in0=cosb[:, js, :], in1=sinb[:, js, :], op=ALU.add)
-            eng.tensor_tensor(out=t2[:, 1, js, :], in0=cosb[:, js, :], in1=sinb[:, js, :], op=ALU.subtract)
+        def tables(eng, lo, hi, q):
+            js = slice(lo, hi)
+            eng.tensor_tensor(out=t2[:, q, js, :], in0=cosb[:, js, :], in1=sinb[:, js, :], op=(ALU.add, ALU.subtract)[q])
 
         wg = const.tile([P, 512, 4], BF16, name="wg", align_bytes=64)
         wc = const.tile([P, 512], U32, name="wc", align_bytes=64)
         ws = const.tile([P, 512], U8, name="ws", align_bytes=64)
 
-        def weights():
+        wt_tiles = []
+
+        def turn_weights():
             for q in range(2):
                 wt = tp_psum.tile([P, 2, 256], F32, name="wt", tag="tp")
                 for tn in range(2):
                     w_words = w_ld[:, tn, 1 - q, :].bitcast(F32)
                     for u in range(2):
                         nc.tensor.transpose(wt[:, u, P * tn : P * (tn + 1)], w_words[:, u:256:2], ident[:])
-                nc.scalar.copy(
-                    out=wg[:, 256 * q : 256 * (q + 1), :]
-                    .rearrange("p c t -> p (c t)")
-                    .bitcast(F32)
-                    .rearrange("p (c u) -> p c u", u=2),
-                    in_=wt[:].rearrange("p u c -> p c u"),
-                )
+                wt_tiles.append(wt)
 
-        for jq in range(NJQ):
-            tables(jq, nc.gpsimd)
+        def group_weights(q, copy):
+            copy(
+                out=wg[:, 256 * q : 256 * (q + 1), :]
+                .rearrange("p c t -> p (c t)")
+                .bitcast(F32)
+                .rearrange("p (c u) -> p c u", u=2),
+                in_=wt_tiles[q][:].rearrange("p u c -> p c u"),
+            )
 
         for gi in range(-4, ng):
             if on_scalar(gi + 2, 1):
                 scale_out(gi + 2, 1)
-            if gi != -3:
-                cast(gi + 4, 0)
-                cast(gi + 4, 1)
+            cast(gi + 4, 0)
+            cast(gi + 4, 1)
             if gi == -4:
-                cast(1, 0)
-                cast(1, 1)
+                for q in range(2):
+                    tables(nc.vector, 0, GT, q)
+                tables(nc.gpsimd, 4, 8, 0)
+                tables(nc.gpsimd, 4, 8, 1)
+                tables(nc.gpsimd, 8, 16, 0)
+                tables(nc.gpsimd, 8, 16, 1)
                 transpose(0, 0)
                 transpose(0, 1)
-                weights()
+                turn_weights()
+                group_weights(0, nc.scalar.copy)
             shared_product(gi, 0)
             multiply_sum(gi + 1, 0)
             rotate(gi, 0)
@@ -296,6 +308,8 @@ def tile_attention_pa_t_kernel(tc, x_bytes, x_scale, wq, wk, freqs_cos, freqs_si
             scale_out(gi + 2, 0)
             if not on_scalar(gi + 2, 1):
                 scale_out(gi + 2, 1)
+            if gi == -2:
+                group_weights(1, nc.vector.tensor_copy)
             if gi > -3:
                 transpose(gi + 3, 0)
                 transpose(gi + 3, 1)

@@ -285,6 +285,8 @@ def tile_attention_pa_t_kernel(tc, x_bytes, x_scale, wq, wk, freqs_cos, freqs_si
             if on_scalar(gi + 2, 1):
                 scale_out(gi + 2, 1)
             cast(gi + 4, 0)
+            if gi == -3:
+                group_weights(0, nc.scalar.copy)
             cast(gi + 4, 1)
             if gi == -4:
                 for q in range(2):
@@ -296,7 +298,6 @@ def tile_attention_pa_t_kernel(tc, x_bytes, x_scale, wq, wk, freqs_cos, freqs_si
                 transpose(0, 0)
                 transpose(0, 1)
                 turn_weights()
-                group_weights(0, nc.scalar.copy)
             shared_product(gi, 0)
             multiply_sum(gi + 1, 0)
             rotate(gi, 0)

@@ -71,10 +71,10 @@ def tile_attention_pa_t_kernel(tc, x_bytes, x_scale, wq, wk, freqs_cos, freqs_si
         nc.sync.dma_start(out=w_ld[:, 0], in_=wq.rearrange("(p par) k -> p par k", par=2))
         nc.sync.dma_start(out=w_ld[:, 1], in_=wk.rearrange("(p par) k -> p par k", par=2))
         load(1, 1)
-        for gi in range(2, 6):
+        for gi in range(2, 7):
             load(gi, 1)
         load_tables(GT, JT)
-        for gi in range(6, ng):
+        for gi in range(7, ng):
             load(gi, 1)
 
         ident = const.tile([P, P], F32, name="ident")
@@ -289,12 +289,12 @@ def tile_attention_pa_t_kernel(tc, x_bytes, x_scale, wq, wk, freqs_cos, freqs_si
                 group_weights(0, nc.scalar.copy)
             cast(gi + 4, 1)
             if gi == -4:
-                for q in range(2):
-                    tables(nc.vector, 0, GT, q)
+                tables(nc.gpsimd, 0, 4, 0)
+                tables(nc.gpsimd, 0, 4, 1)
                 tables(nc.gpsimd, 4, 8, 0)
                 tables(nc.gpsimd, 4, 8, 1)
-                tables(nc.gpsimd, 8, 16, 0)
-                tables(nc.gpsimd, 8, 16, 1)
+                tables(nc.gpsimd, 8, 12, 0)
+                tables(nc.gpsimd, 8, 12, 1)
                 transpose(0, 0)
                 transpose(0, 1)
                 turn_weights()
@@ -325,5 +325,8 @@ def tile_attention_pa_t_kernel(tc, x_bytes, x_scale, wq, wk, freqs_cos, freqs_si
             quantize(gi + 2)
             if live(gi) and not vector_adds(gi, GT // width(gi) - 1):
                 add_and_store(gi, GT // width(gi) - 1)
+                if gi == 0:
+                    tables(nc.gpsimd, 12, 16, 0)
+                    tables(nc.gpsimd, 12, 16, 1)
         for gi, half in ((ng - 2, 1), (ng - 1, 0), (ng - 1, 1)):
             add_and_store(gi, half)

@@ -57,6 +57,7 @@ def tile_attention_pa_t_kernel(tc, x_bytes, x_scale, wq, wk, freqs_cos, freqs_si
             x_tiles.append(x8)
 
         load(0, 2)
+        load(1, 2)
         scl = const.tile([P, 4], F32, name="scl")
         nc.sync.dma_start(out=scl[:], in_=x_scale.rearrange("a b (p t) -> p (a b t)", t=4))
         cosb = const.tile([P, JT, 64], BF16, name="cosb")
@@ -70,7 +71,6 @@ def tile_attention_pa_t_kernel(tc, x_bytes, x_scale, wq, wk, freqs_cos, freqs_si
         w_ld = const.tile([P, 2, 2, D], BF16, name="w_ld")
         nc.sync.dma_start(out=w_ld[:, 0], in_=wq.rearrange("(p par) k -> p par k", par=2))
         nc.sync.dma_start(out=w_ld[:, 1], in_=wk.rearrange("(p par) k -> p par k", par=2))
-        load(1, 1)
         for gi in range(2, 7):
             load(gi, 1)
         load_tables(GT, JT)
@@ -105,7 +105,7 @@ def tile_attention_pa_t_kernel(tc, x_bytes, x_scale, wq, wk, freqs_cos, freqs_si
             if not live(gi):
                 return
             xb = xb_pool.tile([P, 2, D], BF16, name="xb", tag="xb")
-            widen = nc.vector.tensor_copy if (gi, pr) == (0, 0) else nc.scalar.copy
+            widen = nc.vector.tensor_copy if gi == 0 else nc.scalar.copy
             widen(
                 out=xb[:].rearrange("p j k -> p (j k)"),
                 in_=x_tiles[gi][:, 2 * pr : 2 * pr + 2, :].rearrange("p j k -> p (j k)").bitcast(FP8),
@@ -285,9 +285,9 @@ def tile_attention_pa_t_kernel(tc, x_bytes, x_scale, wq, wk, freqs_cos, freqs_si
             if on_scalar(gi + 2, 1):
                 scale_out(gi + 2, 1)
             cast(gi + 4, 0)
+            cast(gi + 4, 1)
             if gi == -3:
                 group_weights(0, nc.scalar.copy)
-            cast(gi + 4, 1)
             if gi == -4:
                 tables(nc.gpsimd, 0, 4, 0)
                 tables(nc.gpsimd, 0, 4, 1)

@@ -99,7 +99,7 @@ def tile_attention_pa_t_kernel(tc, x_bytes, x_scale, wq, wk, freqs_cos, freqs_si
             return (gi, half) >= (ng - 2, 1)
 
         def on_scalar(gi, pr):
-            return pr == 1 and gi >= 2
+            return pr == 1 and gi >= 2 or gi >= 15
 
         def cast(gi, pr):
             if not live(gi):
@@ -263,14 +263,13 @@ def tile_attention_pa_t_kernel(tc, x_bytes, x_scale, wq, wk, freqs_cos, freqs_si
 
         wt_tiles = []
 
-        def turn_weights():
-            for q in range(2):
-                wt = tp_psum.tile([P, 2, 256], F32, name="wt", tag="tp")
-                for tn in range(2):
-                    w_words = w_ld[:, tn, 1 - q, :].bitcast(F32)
-                    for u in range(2):
-                        nc.tensor.transpose(wt[:, u, P * tn : P * (tn + 1)], w_words[:, u:256:2], ident[:])
-                wt_tiles.append(wt)
+        def turn_weights(q):
+            wt = tp_psum.tile([P, 2, 256], F32, name="wt", tag="tp")
+            for tn in range(2):
+                w_words = w_ld[:, tn, 1 - q, :].bitcast(F32)
+                for u in range(2):
+                    nc.tensor.transpose(wt[:, u, P * tn : P * (tn + 1)], w_words[:, u:256:2], ident[:])
+            wt_tiles.append(wt)
 
         def group_weights(q, copy):
             copy(
@@ -282,10 +281,13 @@ def tile_attention_pa_t_kernel(tc, x_bytes, x_scale, wq, wk, freqs_cos, freqs_si
             )
 
         for gi in range(-4, ng):
+            if on_scalar(gi + 2, 0):
+                scale_out(gi + 2, 0)
             if on_scalar(gi + 2, 1):
                 scale_out(gi + 2, 1)
-            cast(gi + 4, 0)
-            cast(gi + 4, 1)
+            if gi != -2:
+                cast(gi + 4, 0)
+                cast(gi + 4, 1)
             if gi == -3:
                 group_weights(0, nc.scalar.copy)
             if gi == -4:
@@ -297,7 +299,7 @@ def tile_attention_pa_t_kernel(tc, x_bytes, x_scale, wq, wk, freqs_cos, freqs_si
                 tables(nc.gpsimd, 8, 12, 1)
                 transpose(0, 0)
                 transpose(0, 1)
-                turn_weights()
+                turn_weights(0)
             shared_product(gi, 0)
             multiply_sum(gi + 1, 0)
             rotate(gi, 0)
@@ -306,18 +308,28 @@ def tile_attention_pa_t_kernel(tc, x_bytes, x_scale, wq, wk, freqs_cos, freqs_si
             multiply(gi + 1, 1)
             if live(gi) and width(gi) == 2 and not vector_adds(gi, 0):
                 add_and_store(gi, 0)
-            scale_out(gi + 2, 0)
+            if gi != -1 and not on_scalar(gi + 2, 0):
+                scale_out(gi + 2, 0)
             if not on_scalar(gi + 2, 1):
                 scale_out(gi + 2, 1)
             if gi == -2:
-                group_weights(1, nc.vector.tensor_copy)
-            if gi > -3:
+                transpose(1, 0)
+                turn_weights(1)
+                group_weights(1, nc.scalar.copy)
+                cast(2, 0)
+                cast(2, 1)
+                transpose(1, 1)
+                scale_out(1, 0)
+            if gi > -2 and not on_scalar(gi + 2, 0):
                 transpose(gi + 3, 0)
                 transpose(gi + 3, 1)
             shared_product(gi, 1)
             multiply_sum(gi + 1, 1)
             rotate(gi, 2)
             multiply(gi + 1, 2)
+            if on_scalar(gi + 2, 0):
+                transpose(gi + 3, 0)
+                transpose(gi + 3, 1)
             rotate(gi, 3)
             multiply(gi + 1, 3)
             if gi == -2:

@@ -29,7 +29,7 @@ def tile_attention_pa_t_kernel(tc, x_bytes, x_scale, wq, wk, freqs_cos, freqs_si
     with ExitStack() as ctx:
         const = ctx.enter_context(tc.tile_pool(name="const", bufs=1))
         bytes_pool = ctx.enter_context(tc.tile_pool(name="bytes", bufs=ng))
-        xb_pool = ctx.enter_context(tc.tile_pool(name="xb", bufs=6))
+        xb_pool = ctx.enter_context(tc.tile_pool(name="xb", bufs=8))
         pl_pool = ctx.enter_context(tc.tile_pool(name="pl", bufs=2))
         xg_pool = ctx.enter_context(tc.tile_pool(name="xg", bufs=2))
         xq_pool = ctx.enter_context(tc.tile_pool(name="xq", bufs=3))
@@ -79,6 +79,8 @@ def tile_attention_pa_t_kernel(tc, x_bytes, x_scale, wq, wk, freqs_cos, freqs_si
 
         ident = const.tile([P, P], F32, name="ident")
         masks.make_identity(nc, ident[:])
+        minus = const.tile([P, P], F32, name="minus")
+        nc.scalar.activation(out=minus[:], in_=ident[:], func=COPY, scale=-1.0)
 
         xb_tiles = {}
         xt_tiles = {}
@@ -88,6 +90,7 @@ def tile_attention_pa_t_kernel(tc, x_bytes, x_scale, wq, wk, freqs_cos, freqs_si
         up_tiles = {}
         p1_tiles = {}
         pm_tiles = {}
+        ost_tiles = {}
 
         def live(gi):
             return 0 <= gi < ng
@@ -98,8 +101,14 @@ def tile_attention_pa_t_kernel(tc, x_bytes, x_scale, wq, wk, freqs_cos, freqs_si
         def vector_adds(gi, half):
             return (gi, half) >= (ng - 2, 1)
 
+        def whole_on_scalar(gi):
+            return gi in (14, 15)
+
+        def tensor_adds(gi):
+            return gi in (13,)
+
         def on_scalar(gi, pr):
-            return pr == 1 and gi >= 2 or gi >= 15
+            return pr == 1 and gi >= 2 or whole_on_scalar(gi)
 
         def cast(gi, pr):
             if not live(gi):
@@ -231,15 +240,38 @@ def tile_attention_pa_t_kernel(tc, x_bytes, x_scale, wq, wk, freqs_cos, freqs_si
                 op=ALU.mult,
             )
 
+        def new_out(gi, half):
+            ost = ost_pool.tile([P, 4, width(gi), P], F32, name="ost", tag="ost")
+            ost_tiles[(gi, half)] = ost
+
+        def tensor_subtract(gi):
+            acc = xt_psum.tile([P, 4, 64, 2], F32, name="xt1", tag="xt1")
+            nc.tensor.matmul(
+                out=acc[:],
+                lhsT=ident[:],
+                rhs=p1_tiles[(gi, 0)][:, :, 0, :].unsqueeze(3).to_broadcast([P, 4, 64, 2]),
+                start=True,
+                stop=False,
+            )
+            nc.tensor.matmul(out=acc[:], lhsT=minus[:], rhs=pm_tiles[(gi, 0)][:, :, 0, :, :], start=False, stop=True)
+            new_out(gi, 0)
+            nc.scalar.copy(out=ost_tiles[(gi, 0)][:, :, 0, :], in_=acc[:].rearrange("p g i q -> p g (i q)"))
+
         def add_and_store(gi, half):
             jq, b = groups[gi]
             w = width(gi)
-            ost = ost_pool.tile([P, 4, w, P], F32, name="ost", tag="ost")
+            if not tensor_adds(gi):
+                new_out(gi, half)
+            ost = ost_tiles[(gi, half)]
+            lo = 64 if tensor_adds(gi) else 0
             eng = nc.vector if vector_adds(gi, half) else nc.gpsimd
             eng.tensor_tensor(
-                out=ost[:].rearrange("p g j (i q) -> p g (j i) q", q=2),
-                in0=p1_tiles[(gi, half)][:].rearrange("p g j i -> p g (j i)").unsqueeze(3).to_broadcast([P, 4, w * 64, 2]),
-                in1=pm_tiles[(gi, half)][:].rearrange("p g j i q -> p g (j i) q"),
+                out=ost[:].rearrange("p g j (i q) -> p g (j i) q", q=2)[:, :, lo:, :],
+                in0=p1_tiles[(gi, half)][:]
+                .rearrange("p g j i -> p g (j i)")[:, :, lo:]
+                .unsqueeze(3)
+                .to_broadcast([P, 4, 64 * w - lo, 2]),
+                in1=pm_tiles[(gi, half)][:].rearrange("p g j i q -> p g (j i) q")[:, :, lo:, :],
                 op=ALU.subtract,
             )
             j_lo = w * half
@@ -280,14 +312,21 @@ def tile_attention_pa_t_kernel(tc, x_bytes, x_scale, wq, wk, freqs_cos, freqs_si
                 in_=wt_tiles[q][:].rearrange("p u c -> p c u"),
             )
 
+        casts = []
+
+        def casts_by(gi):
+            return 2 * (gi + 5) + min(2, max(0, gi - 4))
+
+        def cast_to(n):
+            while len(casts) < min(n, 2 * ng):
+                cast(len(casts) // 2, len(casts) % 2)
+                casts.append(0)
+
         for gi in range(-4, ng):
-            if on_scalar(gi + 2, 0):
-                scale_out(gi + 2, 0)
             if on_scalar(gi + 2, 1):
                 scale_out(gi + 2, 1)
             if gi != -2:
-                cast(gi + 4, 0)
-                cast(gi + 4, 1)
+                cast_to(casts_by(gi))
             if gi == -3:
                 group_weights(0, nc.scalar.copy)
             if gi == -4:
@@ -300,15 +339,22 @@ def tile_attention_pa_t_kernel(tc, x_bytes, x_scale, wq, wk, freqs_cos, freqs_si
                 transpose(0, 0)
                 transpose(0, 1)
                 turn_weights(0)
+            early = whole_on_scalar(gi + 3) and not whole_on_scalar(gi + 2)
+            if early:
+                scale_out(gi + 2, 0)
+                transpose(gi + 3, 0)
+                scale_out(gi + 3, 0)
             shared_product(gi, 0)
             multiply_sum(gi + 1, 0)
             rotate(gi, 0)
             multiply(gi + 1, 0)
             rotate(gi, 1)
             multiply(gi + 1, 1)
+            if tensor_adds(gi):
+                tensor_subtract(gi)
             if live(gi) and width(gi) == 2 and not vector_adds(gi, 0):
                 add_and_store(gi, 0)
-            if gi != -1 and not on_scalar(gi + 2, 0):
+            if gi != -1 and not whole_on_scalar(gi + 2) and not early:
                 scale_out(gi + 2, 0)
             if not on_scalar(gi + 2, 1):
                 scale_out(gi + 2, 1)
@@ -316,20 +362,19 @@ def tile_attention_pa_t_kernel(tc, x_bytes, x_scale, wq, wk, freqs_cos, freqs_si
                 transpose(1, 0)
                 turn_weights(1)
                 group_weights(1, nc.scalar.copy)
-                cast(2, 0)
-                cast(2, 1)
+                cast_to(casts_by(gi))
                 transpose(1, 1)
                 scale_out(1, 0)
-            if gi > -2 and not on_scalar(gi + 2, 0):
-                transpose(gi + 3, 0)
+            if gi > -2:
+                if not early:
+                    transpose(gi + 3, 0)
                 transpose(gi + 3, 1)
+            if whole_on_scalar(gi + 3) and not early:
+                scale_out(gi + 3, 0)
             shared_product(gi, 1)
             multiply_sum(gi + 1, 1)
             rotate(gi, 2)
             multiply(gi + 1, 2)
-            if on_scalar(gi + 2, 0):
-                transpose(gi + 3, 0)
-                transpose(gi + 3, 1)
             rotate(gi, 3)
             multiply(gi + 1, 3)
             if gi == -2:

@@ -99,13 +99,13 @@ def tile_attention_pa_t_kernel(tc, x_bytes, x_scale, wq, wk, freqs_cos, freqs_si
             return GT if 0 < gi < ng - 2 else 2
 
         def vector_adds(gi, half):
-            return (gi, half) >= (ng - 2, 1)
+            return (gi, half) >= (ng - 1, 0)
 
         def whole_on_scalar(gi):
             return gi in (14, 15)
 
         def tensor_adds(gi):
-            return gi in (13,)
+            return gi in (13, 14)
 
         def on_scalar(gi, pr):
             return pr == 1 and gi >= 2 or whole_on_scalar(gi)
@@ -245,7 +245,7 @@ def tile_attention_pa_t_kernel(tc, x_bytes, x_scale, wq, wk, freqs_cos, freqs_si
             ost_tiles[(gi, half)] = ost
 
         def tensor_subtract(gi):
-            acc = xt_psum.tile([P, 4, 64, 2], F32, name="xt1", tag="xt1")
+            acc = xt_psum.tile([P, 4, 64, 2], F32, name="xt0", tag="xt0")
             nc.tensor.matmul(
                 out=acc[:],
                 lhsT=ident[:],
@@ -260,10 +260,11 @@ def tile_attention_pa_t_kernel(tc, x_bytes, x_scale, wq, wk, freqs_cos, freqs_si
         def add_and_store(gi, half):
             jq, b = groups[gi]
             w = width(gi)
-            if not tensor_adds(gi):
+            shared = half == 0 and tensor_adds(gi)
+            if not shared:
                 new_out(gi, half)
             ost = ost_tiles[(gi, half)]
-            lo = 64 if tensor_adds(gi) else 0
+            lo = 64 if shared else 0
             eng = nc.vector if vector_adds(gi, half) else nc.gpsimd
             eng.tensor_tensor(
                 out=ost[:].rearrange("p g j (i q) -> p g (j i) q", q=2)[:, :, lo:, :],
@@ -315,7 +316,7 @@ def tile_attention_pa_t_kernel(tc, x_bytes, x_scale, wq, wk, freqs_cos, freqs_si
         casts = []
 
         def casts_by(gi):
-            return 2 * (gi + 5) + min(2, max(0, gi - 4))
+            return 2 * (gi + 5) + min(2, max(0, gi - 7))
 
         def cast_to(n):
             while len(casts) < min(n, 2 * ng):
@@ -348,10 +349,10 @@ def tile_attention_pa_t_kernel(tc, x_bytes, x_scale, wq, wk, freqs_cos, freqs_si
             multiply_sum(gi + 1, 0)
             rotate(gi, 0)
             multiply(gi + 1, 0)
-            rotate(gi, 1)
-            multiply(gi + 1, 1)
             if tensor_adds(gi):
                 tensor_subtract(gi)
+            rotate(gi, 1)
+            multiply(gi + 1, 1)
             if live(gi) and width(gi) == 2 and not vector_adds(gi, 0):
                 add_and_store(gi, 0)
             if gi != -1 and not whole_on_scalar(gi + 2) and not early:
@@ -385,5 +386,5 @@ def tile_attention_pa_t_kernel(tc, x_bytes, x_scale, wq, wk, freqs_cos, freqs_si
                 if gi == 0:
                     tables(nc.gpsimd, 12, 16, 0)
                     tables(nc.gpsimd, 12, 16, 1)
-        for gi, half in ((ng - 2, 1), (ng - 1, 0), (ng - 1, 1)):
+        for gi, half in ((ng - 1, 0), (ng - 1, 1)):
             add_and_store(gi, half)

from contextlib import ExitStack

import concourse.masks as masks
import concourse.mybir as mybir

F32 = mybir.dt.float32
BF16 = mybir.dt.bfloat16
U32 = mybir.dt.uint32
U8 = mybir.dt.uint8
FP8 = mybir.dt.float8_e4m3fn
FP8X4 = mybir.dt.float8_e4m3fn_x4
ALU = mybir.AluOpType
COPY = mybir.ActivationFunctionType.Copy

B, S, D = 4, 2048, 512
P = 128
JT = S // P
GT = 4
NJQ = JT // GT
FLOPS = 2 * B * S * D * 512


def tile_attention_pa_t_kernel(tc, x_bytes, x_scale, wq, wk, freqs_cos, freqs_sin, out_0, out_1):
    nc = tc.nc
    outs = (out_0, out_1)
    groups = [(jq, b) for jq in range(NJQ) for b in range(B)]
    ng = len(groups)

    with ExitStack() as ctx:
        const = ctx.enter_context(tc.tile_pool(name="const", bufs=1))
        bytes_pool = ctx.enter_context(tc.tile_pool(name="bytes", bufs=ng))
        xb_pool = ctx.enter_context(tc.tile_pool(name="xb", bufs=8))
        pl_pool = ctx.enter_context(tc.tile_pool(name="pl", bufs=2))
        xg_pool = ctx.enter_context(tc.tile_pool(name="xg", bufs=2))
        xq_pool = ctx.enter_context(tc.tile_pool(name="xq", bufs=3))
        pm_pool = ctx.enter_context(tc.tile_pool(name="pm", bufs=5))
        p1_pool = ctx.enter_context(tc.tile_pool(name="p1", bufs=5))
        ost_pool = ctx.enter_context(tc.tile_pool(name="ost", bufs=5))
        xt_psum = ctx.enter_context(tc.psum_pool(name="xtp", bufs=1))
        tp_psum = ctx.enter_context(tc.psum_pool(name="tpp", bufs=4))
        up_psum = ctx.enter_context(tc.psum_pool(name="upp", bufs=2))
        ctx.enter_context(tc.manual_schedule())

        x_tiles = []

        def load(gi, pieces):
            jq, b = groups[gi]
            x8 = bytes_pool.tile([P, GT, D], U8, name="x8", tag="x8")
            step = GT // pieces
            for c in range(pieces):
                nc.sync.dma_start(
                    out=x8[:, step * c : step * (c + 1), :],
                    in_=x_bytes[b].rearrange("(p j) k -> p j k", j=JT)[
                        :, GT * jq + step * c : GT * jq + step * (c + 1), :
                    ],
                )
            x_tiles.append(x8)

        load(0, 2)
        load(1, 2)
        scl = const.tile([P, 4], F32, name="scl")
        nc.sync.dma_start(out=scl[:], in_=x_scale.rearrange("a b (p t) -> p (a b t)", t=4))
        cosb = const.tile([P, JT, 64], BF16, name="cosb")
        sinb = const.tile([P, JT, 64], BF16, name="sinb")

        def load_tables(lo, hi):
            nc.sync.dma_start(out=cosb[:, lo:hi, :], in_=freqs_cos.rearrange("(p j) i -> p j i", j=JT)[:, lo:hi, :])
            nc.sync.dma_start(out=sinb[:, lo:hi, :], in_=freqs_sin.rearrange("(p j) i -> p j i", j=JT)[:, lo:hi, :])

        load_tables(0, GT)
        w_ld = const.tile([P, 2, 2, D], BF16, name="w_ld")
        nc.sync.dma_start(out=w_ld[:, 0], in_=wq.rearrange("(p par) k -> p par k", par=2))
        nc.sync.dma_start(out=w_ld[:, 1], in_=wk.rearrange("(p par) k -> p par k", par=2))
        for gi in range(2, 7):
            load(gi, 1)
        load_tables(GT, JT)
        for gi in range(7, ng):
            load(gi, 1)

        ident = const.tile([P, P], F32, name="ident")
        masks.make_identity(nc, ident[:])
        minus = const.tile([P, P], F32, name="minus")
        nc.scalar.activation(out=minus[:], in_=ident[:], func=COPY, scale=-1.0)

        xb_tiles = {}
        xt_tiles = {}
        xg_tiles = {}
        xq_tiles = {}
        tp_tiles = {}
        up_tiles = {}
        p1_tiles = {}
        pm_tiles = {}
        ost_tiles = {}

        def live(gi):
            return 0 <= gi < ng

        def width(gi):
            return GT if 0 < gi < ng - 2 else 2

        def vector_adds(gi, half):
            return (gi, half) >= (ng - 1, 0)

        def whole_on_scalar(gi):
            return gi in (14, 15)

        def tensor_adds(gi):
            return gi in (13, 14)

        def on_scalar(gi, pr):
            return pr == 1 and gi >= 2 or whole_on_scalar(gi)

        def cast(gi, pr):
            if not live(gi):
                return
            xb = xb_pool.tile([P, 2, D], BF16, name="xb", tag="xb")
            widen = nc.vector.tensor_copy if gi == 0 else nc.scalar.copy
            widen(
                out=xb[:].rearrange("p j k -> p (j k)"),
                in_=x_tiles[gi][:, 2 * pr : 2 * pr + 2, :].rearrange("p j k -> p (j k)").bitcast(FP8),
            )
            xb_tiles[(gi, pr)] = xb

        def transpose(gi, pr):
            if not live(gi):
                return
            words = xb_tiles[(gi, pr)][:].rearrange("p j k -> p (j k)").bitcast(F32)
            xt = xt_psum.tile([P, 2, 2, P], F32, name="xt%d" % pr, tag="xt%d" % pr)
            for jp in range(2):
                for u in range(2):
                    nc.tensor.transpose(xt[:, u, jp, :], words[:, 256 * jp + u : 256 * (jp + 1) : 2], ident[:])
            xt_tiles[(gi, pr)] = xt

        def scale_out(gi, pr):
            if not live(gi):
                return
            if gi not in xg_tiles:
                xg_new = xg_pool.tile([P, GT, P, 4], BF16, name="xg", tag="xg", align_bytes=64)
                xg_tiles[gi] = xg_new
            xg = xg_tiles[gi]
            xt = xt_tiles[(gi, pr)]
            src = xt[:].rearrange("p u j r -> p u (j r)").bitcast(BF16).rearrange("p u (c e) -> p u c e", e=2)
            dst = xg[:, 2 * pr : 2 * pr + 2, :, :].rearrange("p j r t -> p (j r) t")
            if on_scalar(gi, pr):
                pl = pl_pool.tile([P, 4, 2 * P], BF16, name="pl", tag="pl")
                for t in range(4):
                    nc.scalar.activation(
                        out=pl[:, t, :], in_=src[:, t // 2, :, t % 2], func=COPY, scale=scl[:, t : t + 1]
                    )
                nc.scalar.copy(
                    out=dst.rearrange("p (c i) t -> p c t i", i=4), in_=pl[:].rearrange("p t (c i) -> p c t i", i=4)
                )
            else:
                nc.vector.tensor_tensor(
                    out=dst.rearrange("p c (u e) -> p c u e", e=2),
                    in0=src.rearrange("p u c e -> p c u e"),
                    in1=scl[:].rearrange("p (u e) -> p u e", e=2).unsqueeze(1).to_broadcast([P, 2 * P, 2, 2]),
                    op=ALU.mult,
                )

        def quantize(gi):
            if not live(gi):
                return
            xc = xq_pool.tile([P, GT * P], U32, name="xc", tag="xc", align_bytes=64)
            xs = xq_pool.tile([P, GT * P], U8, name="xs", tag="xs", align_bytes=64)
            nc.vector.quantize_mx(
                out=xc[:].bitcast(FP8X4),
                scales=xs[:],
                in_=xg_tiles[gi][:].rearrange("p j r t -> p (j r t)"),
            )
            xq_tiles[gi] = (xc, xs)

        def multiply_sum(gi, pr):
            if not live(gi):
                return
            xc, xs = xq_tiles[gi]
            up = up_psum.tile([P, 2, 256], F32, name="up", tag="up")
            up_tiles[(gi, pr)] = up
            for jp in range(2):
                cols = slice(P * (2 * pr + jp), P * (2 * pr + jp + 1))
                for half in range(2):
                    nc.tensor.matmul_mx(
                        out=up[:, jp, :],
                        lhsT=xc[:, cols].bitcast(FP8X4),
                        lhsT_scale=xs[:, cols],
                        rhs=wc[:, 256 * half : 256 * (half + 1)].bitcast(FP8X4),
                        rhs_scale=ws[:, 256 * half : 256 * (half + 1)],
                        start=(half == 0),
                        stop=(half == 1),
                    )

        def multiply(gi, jj):
            if not live(gi):
                return
            xc, xs = xq_tiles[gi]
            cols = slice(P * jj, P * (jj + 1))
            tp = tp_psum.tile([P, 512], F32, name="tp", tag="tp")
            tp_tiles[(gi, jj)] = tp
            nc.tensor.matmul_mx(
                out=tp[:],
                lhsT=xc[:, cols].bitcast(FP8X4),
                lhsT_scale=xs[:, cols],
                rhs=wc[:].bitcast(FP8X4),
                rhs_scale=ws[:],
                start=True,
                stop=True,
            )

        def shared_product(gi, pr):
            if not live(gi):
                return
            jq, b = groups[gi]
            j0 = GT * jq + 2 * pr
            w = width(gi)
            if (2 * pr) % w == 0:
                p1_new = p1_pool.tile([P, 4, w, 64], F32, name="p1", tag="p1")
                p1_tiles[(gi, 2 * pr // w)] = p1_new
            p1 = p1_tiles[(gi, 2 * pr // w)]
            jl = (2 * pr) % w
            nc.vector.tensor_tensor(
                out=p1[:, :, jl : jl + 2, :].rearrange("p g j i -> p j g i"),
                in0=up_tiles[(gi, pr)][:].rearrange("p j (g i) -> p j g i", g=4),
                in1=cosb[:, j0 : j0 + 2, :].unsqueeze(2).to_broadcast([P, 2, 4, 64]),
                op=ALU.mult,
            )

        def rotate(gi, jj):
            if not live(gi):
                return
            jq, b = groups[gi]
            w = width(gi)
            if jj % w == 0:
                pm_new = pm_pool.tile([P, 4, w, 64, 2], F32, name="pm", tag="pm")
                pm_tiles[(gi, jj // w)] = pm_new
            pm = pm_tiles[(gi, jj // w)]
            nc.vector.tensor_tensor(
                out=pm[:, :, jj % w, :, :],
                in0=tp_tiles[(gi, jj)][:].rearrange("p (q g i) -> p g i q", q=2, g=4),
                in1=t2[:, :, GT * jq + jj, :].rearrange("p q i -> p i q").unsqueeze(1).to_broadcast([P, 4, 64, 2]),
                op=ALU.mult,
            )

        def new_out(gi, half):
            ost = ost_pool.tile([P, 4, width(gi), P], F32, name="ost", tag="ost")
            ost_tiles[(gi, half)] = ost

        def tensor_subtract(gi):
            acc = xt_psum.tile([P, 4, 64, 2], F32, name="xt0", tag="xt0")
            nc.tensor.matmul(
                out=acc[:],
                lhsT=ident[:],
                rhs=p1_tiles[(gi, 0)][:, :, 0, :].unsqueeze(3).to_broadcast([P, 4, 64, 2]),
                start=True,
                stop=False,
            )
            nc.tensor.matmul(out=acc[:], lhsT=minus[:], rhs=pm_tiles[(gi, 0)][:, :, 0, :, :], start=False, stop=True)
            new_out(gi, 0)
            nc.scalar.copy(out=ost_tiles[(gi, 0)][:, :, 0, :], in_=acc[:].rearrange("p g i q -> p g (i q)"))

        def add_and_store(gi, half):
            jq, b = groups[gi]
            w = width(gi)
            shared = half == 0 and tensor_adds(gi)
            if not shared:
                new_out(gi, half)
            ost = ost_tiles[(gi, half)]
            lo = 64 if shared else 0
            eng = nc.vector if vector_adds(gi, half) else nc.gpsimd
            eng.tensor_tensor(
                out=ost[:].rearrange("p g j (i q) -> p g (j i) q", q=2)[:, :, lo:, :],
                in0=p1_tiles[(gi, half)][:]
                .rearrange("p g j i -> p g (j i)")[:, :, lo:]
                .unsqueeze(3)
                .to_broadcast([P, 4, 64 * w - lo, 2]),
                in1=pm_tiles[(gi, half)][:].rearrange("p g j i q -> p g (j i) q")[:, :, lo:, :],
                op=ALU.subtract,
            )
            j_lo = w * half
            j_hi = w * (half + 1)
            for tn in range(2):
                queue = nc.scalar if tn == 1 and vector_adds(gi, half) else nc.sync
                queue.dma_start(
                    out=outs[tn][b].rearrange("h (p j) d -> p h j d", j=JT)[:, :, GT * jq + j_lo : GT * jq + j_hi, :],
                    in_=ost[:, 2 * tn : 2 * tn + 2, :, :],
                )

        t2 = const.tile([P, 2, JT, 64], F32, name="t2")

        def tables(eng, lo, hi, q):
            js = slice(lo, hi)
            eng.tensor_tensor(out=t2[:, q, js, :], in0=cosb[:, js, :], in1=sinb[:, js, :], op=(ALU.add, ALU.subtract)[q])

        wg = const.tile([P, 512, 4], BF16, name="wg", align_bytes=64)
        wc = const.tile([P, 512], U32, name="wc", align_bytes=64)
        ws = const.tile([P, 512], U8, name="ws", align_bytes=64)

        wt_tiles = []

        def turn_weights(q):
            wt = tp_psum.tile([P, 2, 256], F32, name="wt", tag="tp")
            for tn in range(2):
                w_words = w_ld[:, tn, 1 - q, :].bitcast(F32)
                for u in range(2):
                    nc.tensor.transpose(wt[:, u, P * tn : P * (tn + 1)], w_words[:, u:256:2], ident[:])
            wt_tiles.append(wt)

        def group_weights(q, copy):
            copy(
                out=wg[:, 256 * q : 256 * (q + 1), :]
                .rearrange("p c t -> p (c t)")
                .bitcast(F32)
                .rearrange("p (c u) -> p c u", u=2),
                in_=wt_tiles[q][:].rearrange("p u c -> p c u"),
            )

        casts = []

        def casts_by(gi):
            return 2 * (gi + 5) + min(2, max(0, gi - 7))

        def cast_to(n):
            while len(casts) < min(n, 2 * ng):
                cast(len(casts) // 2, len(casts) % 2)
                casts.append(0)

        for gi in range(-4, ng):
            if on_scalar(gi + 2, 1):
                scale_out(gi + 2, 1)
            if gi != -2:
                cast_to(casts_by(gi))
            if gi == -3:
                group_weights(0, nc.scalar.copy)
            if gi == -4:
                tables(nc.gpsimd, 0, 4, 0)
                tables(nc.gpsimd, 0, 4, 1)
                tables(nc.gpsimd, 4, 8, 0)
                tables(nc.gpsimd, 4, 8, 1)
                tables(nc.gpsimd, 8, 12, 0)
                tables(nc.gpsimd, 8, 12, 1)
                transpose(0, 0)
                transpose(0, 1)
                turn_weights(0)
            early = whole_on_scalar(gi + 3) and not whole_on_scalar(gi + 2)
            if early:
                scale_out(gi + 2, 0)
                transpose(gi + 3, 0)
                scale_out(gi + 3, 0)
            shared_product(gi, 0)
            multiply_sum(gi + 1, 0)
            rotate(gi, 0)
            multiply(gi + 1, 0)
            if tensor_adds(gi):
                tensor_subtract(gi)
            rotate(gi, 1)
            multiply(gi + 1, 1)
            if live(gi) and width(gi) == 2 and not vector_adds(gi, 0):
                add_and_store(gi, 0)
            if gi != -1 and not whole_on_scalar(gi + 2) and not early:
                scale_out(gi + 2, 0)
            if not on_scalar(gi + 2, 1):
                scale_out(gi + 2, 1)
            if gi == -2:
                transpose(1, 0)
                turn_weights(1)
                group_weights(1, nc.scalar.copy)
                cast_to(casts_by(gi))
                transpose(1, 1)
                scale_out(1, 0)
            if gi > -2:
                if not early:
                    transpose(gi + 3, 0)
                transpose(gi + 3, 1)
            if whole_on_scalar(gi + 3) and not early:
                scale_out(gi + 3, 0)
            shared_product(gi, 1)
            multiply_sum(gi + 1, 1)
            rotate(gi, 2)
            multiply(gi + 1, 2)
            rotate(gi, 3)
            multiply(gi + 1, 3)
            if gi == -2:
                nc.vector.quantize_mx(out=wc[:].bitcast(FP8X4), scales=ws[:], in_=wg[:].rearrange("p c t -> p (c t)"))
            quantize(gi + 2)
            if live(gi) and not vector_adds(gi, GT // width(gi) - 1):
                add_and_store(gi, GT // width(gi) - 1)
                if gi == 0:
                    tables(nc.gpsimd, 12, 16, 0)
                    tables(nc.gpsimd, 12, 16, 1)
        for gi, half in ((ng - 1, 0), (ng - 1, 1)):
            add_and_store(gi, half)
